import numpy as np
import ml_dtypes


def mxq(x, axis, fmt="e4m3"):
    dtype, down = {"e4m3": (ml_dtypes.float8_e4m3fn, 7), "e5m2": (ml_dtypes.float8_e5m2, 14)}[fmt]
    v = np.moveaxis(np.asarray(x, np.float32).astype(ml_dtypes.bfloat16).astype(np.float64), axis, -1)
    blocks = v.reshape(v.shape[:-1] + (-1, 32))
    amax = np.abs(blocks).max(-1, keepdims=True)
    byte = np.maximum(np.where(amax > 0, np.frexp(amax)[1] - 1 + 127, 0) - down, 1)
    scale = np.exp2(byte - 127.0)
    codes = (blocks / scale).astype(np.float32).astype(dtype).astype(np.float64)
    return np.moveaxis((codes * scale).reshape(v.shape), -1, axis)


WIDE = False


def mx_kscale(k):
    if not WIDE:
        return np.ones(k)
    levels = np.array([30, -30])
    if k % 512:
        return np.exp2(np.random.permutation(np.resize(levels, k // 32))).repeat(32)
    a = np.empty((k // 512, 16))
    for p in range(k // 512):
        a[p, :8] = np.random.permutation(np.resize(levels, 8))
        for g in range(8):
            far = levels[np.abs(levels - a[p, g]) >= 10]
            a[p, g + 8] = far[np.random.randint(len(far))]
    return np.exp2(a.ravel()).repeat(32)


BF16 = ml_dtypes.bfloat16


def bf(x):
    return np.asarray(x, np.float32).astype(BF16)


def f64(x):
    return np.asarray(x).astype(np.float64)


B, S, D, NH, HS, ROT = 2, 512, 1024, 8, 128, 32
BASE = 10000.0
HALF = ROT // 2
W3 = 3 * NH * HS


def rotate_half(x):
    return np.concatenate([-x[..., HALF:], x[..., :HALF]], axis=-1)


def rope_tables():
    inv_freq = 1.0 / BASE ** (np.arange(0, ROT, 2) / ROT)
    freqs = np.outer(np.arange(S), inv_freq)
    emb = np.concatenate([freqs, freqs], axis=-1)
    return np.cos(emb)[None, None], np.sin(emb)[None, None]


def apply_rot(x, cos, sin):
    xr, xp = x[..., :ROT], x[..., ROT:]
    xr = xr * cos + rotate_half(xr) * sin
    return np.concatenate([xr, xp], axis=-1)


def setup_inputs():
    s = mx_kscale(D)
    return {"hidden_states": bf(np.random.standard_normal((B, S, D)) * s),
            "w_qkv": bf(np.random.standard_normal((D, W3)) * 1.5 / np.sqrt(D) / s[:, None])}


def reference(hidden_states, w_qkv):
    qkv = mxq(f64(hidden_states), 2, "e5m2") @ mxq(f64(w_qkv), 0, "e5m2")
    qkv = qkv.reshape(B, S, NH, 3 * HS)
    q = qkv[..., :HS].transpose(0, 2, 1, 3)
    k = qkv[..., HS:2 * HS].transpose(0, 2, 1, 3)
    v = qkv[..., 2 * HS:].transpose(0, 2, 1, 3)
    cos, sin = rope_tables()
    return apply_rot(q, cos, sin), apply_rot(k, cos, sin), v

@@ -1,0 +1,198 @@
+import math
+from contextlib import ExitStack
+
+import concourse.mybir as mybir
+from concourse.masks import make_identity
+
+B, S, D, NH, HS, ROT = 2, 512, 1024, 8, 128, 32
+HALF = ROT // 2
+BASE = 10000.0
+FLOPS = 2 * B * S * D * 3 * NH * HS
+
+F32 = mybir.dt.float32
+BF16 = mybir.dt.bfloat16
+I32 = mybir.dt.int32
+U32 = mybir.dt.uint32
+U8 = mybir.dt.uint8
+FP8X4 = mybir.dt.float8_e5m2_x4
+ALU = mybir.AluOpType
+ACT = mybir.ActivationFunctionType
+
+P = 128
+G = 2
+MT = 4
+CH = 768
+
+
+def tile_gptneoxjapaneseattention_pa_kernel(tc, hidden_states, w_qkv, out_0, out_1, out_2):
+    nc = tc.nc
+    with ExitStack() as ctx:
+        keep = ctx.enter_context(tc.tile_pool(name="keep", bufs=1))
+        xg_pool = ctx.enter_context(tc.tile_pool(name="xg", bufs=4))
+        wg_pool = ctx.enter_context(tc.tile_pool(name="wg", bufs=4))
+        o_pool = ctx.enter_context(tc.tile_pool(name="o", bufs=10))
+        bt_pool = ctx.enter_context(tc.tile_pool(name="bt", bufs=3))
+        psum = ctx.enter_context(tc.psum_pool(name="psum", bufs=8))
+
+        zero = keep.tile([P, 1], F32, name="zero")
+        nc.gpsimd.memset(zero[:], 0.0)
+        warm = keep.tile([P, 1], F32, name="warm")
+        nc.scalar.activation(out=warm[:], in_=zero[:], func=ACT.Sin)
+
+        xraw = [keep.tile([P, MT, D], BF16, name="xraw%d" % b) for b in range(B)]
+        wraw = [[keep.tile([P, 4, CH], BF16, name="wraw%d_%d" % (a, g)) for g in range(G)] for a in range(4)]
+
+        def load_x(b):
+            src = hidden_states[b].rearrange("(p m) k -> p m k", m=MT)
+            for h in range(2):
+                nc.sync.dma_start(out=xraw[b][:, 2 * h : 2 * h + 2, :], in_=src[:, 2 * h : 2 * h + 2, :])
+
+        def load_w(a):
+            for g in range(G):
+                nc.sync.dma_start(
+                    out=wraw[a][g][:],
+                    in_=w_qkv[512 * g : 512 * (g + 1), CH * a : CH * (a + 1)].rearrange("(p j) w -> p j w", j=4),
+                )
+
+        load_x(0)
+        load_w(0)
+        load_x(1)
+        load_w(1)
+        load_w(2)
+        load_w(3)
+
+        ident = keep.tile([P, P], F32, name="ident")
+        make_identity(nc, ident[:])
+
+        W = MT * ROT
+        pos = keep.tile([P, W], F32, name="pos")
+        nc.gpsimd.iota(pos[:], pattern=[[1, MT], [0, ROT]], base=0, channel_multiplier=MT,
+                       allow_small_or_imprecise_dtypes=True)
+        turns = keep.tile([P, W], F32, name="turns")
+        pos_v = pos[:].rearrange("p (a j) -> p a j", j=HALF)
+        turns_v = turns[:].rearrange("p (a j) -> p a j", j=HALF)
+        for j in range(HALF):
+            c_j = 1.0 / (BASE ** (2.0 * j / ROT)) / (2.0 * math.pi)
+            nc.vector.tensor_scalar(out=turns_v[:, :, j : j + 1], in0=pos_v[:, :, j : j + 1],
+                                    scalar1=c_j, scalar2=None, op0=ALU.mult)
+        whole_i = keep.tile([P, W], I32, name="whole_i")
+        nc.vector.tensor_copy(out=whole_i[:], in_=turns[:])
+        whole_f = keep.tile([P, W], F32, name="whole_f")
+        nc.vector.tensor_copy(out=whole_f[:], in_=whole_i[:])
+        frac = keep.tile([P, W], F32, name="frac")
+        nc.vector.tensor_tensor(out=frac[:], in0=turns[:], in1=whole_f[:], op=ALU.subtract)
+        s_half = keep.tile([P, W], F32, name="s_half")
+        nc.scalar.activation(out=s_half[:], in_=frac[:], func=ACT.Sin, scale=math.pi)
+        s_quar = keep.tile([P, W], F32, name="s_quar")
+        nc.scalar.activation(out=s_quar[:], in_=frac[:], func=ACT.Sin, scale=math.pi / 2.0)
+        sq = keep.tile([P, W], F32, name="sq")
+        nc.vector.tensor_tensor(out=sq[:], in0=s_half[:], in1=s_half[:], op=ALU.mult)
+        cos_t = keep.tile([P, MT, ROT], F32, name="cos_t")
+        nc.vector.tensor_scalar(out=cos_t[:].rearrange("p m r -> p (m r)"), in0=sq[:],
+                                scalar1=-2.0, scalar2=1.0, op0=ALU.mult, op1=ALU.add)
+        sq2 = keep.tile([P, W], F32, name="sq2")
+        nc.vector.tensor_tensor(out=sq2[:], in0=s_quar[:], in1=s_quar[:], op=ALU.mult)
+        c_half = keep.tile([P, W], F32, name="c_half")
+        nc.vector.tensor_scalar(out=c_half[:], in0=sq2[:], scalar1=-2.0, scalar2=1.0, op0=ALU.mult, op1=ALU.add)
+        sin_t = keep.tile([P, MT, ROT], F32, name="sin_t")
+        sh_v = s_half[:].rearrange("p (m h j) -> p m h j", m=MT, h=2)
+        ch_v = c_half[:].rearrange("p (m h j) -> p m h j", m=MT, h=2)
+        st_v = sin_t[:].rearrange("p m (h j) -> p m h j", h=2)
+        for h, sign in ((0, 2.0), (1, -2.0)):
+            nc.vector.scalar_tensor_tensor(out=st_v[:, :, h, :], in0=sh_v[:, :, h, :], scalar=sign,
+                                           in1=ch_v[:, :, h, :], op0=ALU.mult, op1=ALU.mult)
+
+        xcodes = [keep.tile([P, MT, G, P], U32, name="xcodes%d" % b, align_bytes=64) for b in range(B)]
+        xscales = [keep.tile([P, MT, G, P], U8, name="xscales%d" % b, align_bytes=64) for b in range(B)]
+
+        def prep_x(b):
+            for m in range(MT):
+                words = xraw[b][:, m, :].bitcast(F32)
+                xt = psum.tile([P, G, 2, P], F32, tag="bank", name="xt")
+                for g in range(G):
+                    for u in range(2):
+                        nc.tensor.transpose(xt[:, g, u, :], words[:, 256 * g + u : 256 * (g + 1) : 2], ident[:])
+                xg = xg_pool.tile([P, G, P, 4], BF16, name="xg", align_bytes=64)
+                nc.scalar.copy(out=xg[:].bitcast(F32), in_=xt[:].rearrange("p g u r -> p g r u"))
+                nc.vector.quantize_mx(
+                    out=xcodes[b][:, m].rearrange("p g r -> p (g r)").bitcast(FP8X4),
+                    scales=xscales[b][:, m].rearrange("p g r -> p (g r)"),
+                    in_=xg[:].rearrange("p g r t -> p (g r t)"),
+                )
+
+        tiles = [("qk", 0), ("qk", 1), ("v", 0), ("qk", 2), ("qk", 3), ("v", 1)]
+        wcodes = [keep.tile([P, G, 512], U32, name="wcodes%d" % i, align_bytes=64) for i in range(6)]
+        wscales = [keep.tile([P, G, 512], U8, name="wscales%d" % i, align_bytes=64) for i in range(6)]
+
+        def interleave(on_vector, dst, src):
+            if on_vector:
+                nc.vector.tensor_copy(out=dst, in_=src.rearrange("p j w -> p w j"))
+            else:
+                nc.scalar.copy(out=dst, in_=src.rearrange("p j w -> p w j"))
+
+        def prep_w(i):
+            kind, a = tiles[i]
+            for g in range(G):
+                wg = wg_pool.tile([P, 512, 4], BF16, name="wg", align_bytes=64)
+                if kind == "qk":
+                    for hh in range(2):
+                        interleave(not (hh == 1 and g == 1), wg[:, 256 * hh : 256 * (hh + 1), :],
+                                   wraw[a][g][:, :, 384 * hh : 384 * hh + 256])
+                else:
+                    for u in range(4):
+                        interleave(u < 2 or (u == 2 and g == 0), wg[:, 128 * u : 128 * (u + 1), :],
+                                   wraw[2 * a + u // 2][g][:, :, 384 * (u % 2) + 256 : 384 * (u % 2) + 384])
+                nc.vector.quantize_mx(
+                    out=wcodes[i][:, g, :].bitcast(FP8X4),
+                    scales=wscales[i][:, g, :],
+                    in_=wg[:].rearrange("p w j -> p (w j)"),
+                )
+
+        def product(i, b):
+            kind, a = tiles[i]
+            osb = o_pool.tile([P, 4, MT, HS], F32, name="osb")
+            bt = None
+            if kind == "qk":
+                bt = bt_pool.tile([P, 4, MT, ROT], F32, name="bt")
+            for m in range(MT):
+                ps = psum.tile([P, 4, HS], F32, tag="bank", name="ps")
+                for g in range(G):
+                    nc.tensor.matmul_mx(
+                        out=ps[:].rearrange("p u f -> p (u f)"),
+                        lhsT=xcodes[b][:, m, g, :].bitcast(FP8X4),
+                        lhsT_scale=xscales[b][:, m, g, :],
+                        rhs=wcodes[i][:, g, :].bitcast(FP8X4),
+                        rhs_scale=wscales[i][:, g, :],
+                        start=(g == 0),
+                        stop=(g == G - 1),
+                    )
+                if kind == "qk":
+                    nc.vector.tensor_tensor(out=osb[:, :, m, 0:ROT], in0=ps[:, :, 0:ROT],
+                                            in1=cos_t[:, m : m + 1, :].to_broadcast([P, 4, ROT]), op=ALU.mult)
+                    nc.vector.tensor_tensor(out=bt[:, :, m, :], in0=ps[:, :, 0:ROT],
+                                            in1=sin_t[:, m : m + 1, :].to_broadcast([P, 4, ROT]), op=ALU.mult)
+                    nc.scalar.copy(out=osb[:, :, m, ROT:HS], in_=ps[:, :, ROT:HS])
+                else:
+                    nc.scalar.copy(out=osb[:, :, m, :], in_=ps[:])
+            if kind == "qk":
+                nc.vector.tensor_tensor(out=osb[:, :, :, 0:HALF], in0=osb[:, :, :, 0:HALF],
+                                        in1=bt[:, :, :, HALF:ROT], op=ALU.add)
+                nc.vector.tensor_tensor(out=osb[:, :, :, HALF:ROT], in0=osb[:, :, :, HALF:ROT],
+                                        in1=bt[:, :, :, 0:HALF], op=ALU.add)
+                by_kind = osb[:].rearrange("p (hh s) m f -> p s hh (m f)", s=2)
+                for s, dst in ((0, out_0), (1, out_1)):
+                    nc.sync.dma_start(out=dst[b, 2 * a : 2 * a + 2].rearrange("h (p m) f -> p h (m f)", m=MT),
+                                      in_=by_kind[:, s])
+            else:
+                nc.sync.dma_start(out=out_2[b, 4 * a : 4 * a + 4].rearrange("h (p m) f -> p h (m f)", m=MT),
+                                  in_=osb[:].rearrange("p u m f -> p u (m f)"))
+
+        prep_x(0)
+        prep_w(0)
+        for i in range(6):
+            if i + 1 < 6:
+                prep_w(i + 1)
+            product(i, 0)
+            if i == 0:
+                prep_x(1)
+            product(i, 1)

@@ -125,10 +125,12 @@ def tile_gptneoxjapaneseattention_pa_kernel(tc, hidden_states, w_qkv, out_0, out
         wscales = [keep.tile([P, G, 512], U8, name="wscales%d" % i, align_bytes=64) for i in range(6)]
 
         def interleave(on_vector, dst, src):
+            d = dst.rearrange("p (c i) j -> p c j i", i=4)
+            s = src.rearrange("p j (c i) -> p c j i", i=4)
             if on_vector:
-                nc.vector.tensor_copy(out=dst, in_=src.rearrange("p j w -> p w j"))
+                nc.vector.tensor_copy(out=d, in_=s)
             else:
-                nc.scalar.copy(out=dst, in_=src.rearrange("p j w -> p w j"))
+                nc.scalar.copy(out=d, in_=s)
 
         def prep_w(i):
             kind, a = tiles[i]

@@ -22,6 +22,145 @@ P = 128
 G = 2
 MT = 4
 CH = 768
+NWG = 6
+
+TILES = [("qk", 0), ("qk", 1), ("v", 0), ("qk", 2), ("v", 1), ("qk", 3)]
+SHARE = [192, 192, 128, 128, 256, 256, 256, 256, 128, 128, 256, 256]
+Q_PE = """tx0 mm0 tx1 mm1 mm2 mm3 mm4 mm5 mm6 mm7 mm8 mm9 mm10 mm11"""
+Q_V = """tab1 tab2 iv-2 qx0.01 iv-1 qw-2 qw-1 qx0.23
+ rm0 iv0 ra0 qx1.01 iv1 qx1.23 qw0 qw1
+ rm1 iv2 ra1 iv3 qw2
+ rm2 qw3 ra2 iv4
+ rm3 iv5 ra3 qw4 qw5
+ iv6 iv7 qw6 qw7
+ rm6 iv8 ra6 iv9
+ rm7 qw8 ra7 qw9
+ cv8.13 cv9.13
+ rm10 ra10 rm11 ra11"""
+Q_S = """warm sin ex0.01 is-2 is-1 ex0.23
+ cp0 ex1 is0 is1 is2 is3 cp1 cp2 is4 is5 cp3 cp4 is6 is7 cp5 is8 is9 cp6 cp7 cp8.02 cp9.02 cp10 cp11"""
+Q_SP = """lx00 lw00 lw01 lx01 lx10 lx11 lw10 lw11 lw20 lw21 lw30 lw31 st0 st1 st2 st3 st4 st5 st6 st7 st8 st9 st10 st11"""
+
+
+def unit(u):
+    return (1 + u // 2, u % 2) if u >= 0 else (0, u + 2)
+
+
+def parse(txt):
+    out = []
+    for w in txt.split():
+        k = w[:2]
+        rest = w[2:]
+        if k in ("rm", "cp", "mm", "cv"):
+            ms = list(range(4))
+            if "." in rest:
+                ms = [int(c) for c in rest.split(".")[1]]
+                rest = rest.split(".")[0]
+            p = int(rest)
+            for m in ms:
+                if k == "cp":
+                    out.append(("cp", p // 2, p % 2, m, "S"))
+                elif k == "cv":
+                    out.append(("cp", p // 2, p % 2, m, "V"))
+                else:
+                    out.append((k, p // 2, p % 2, m))
+        elif k in ("ra", "st"):
+            out.append((k, int(rest) // 2, int(rest) % 2))
+        elif k in ("tx", "ex", "qx"):
+            ms = list(range(4))
+            if "." in rest:
+                ms = [int(c) for c in rest.split(".")[1]]
+            out.extend([(k, int(rest[0]), m) for m in ms])
+        elif k in ("iv", "is", "qw"):
+            out.append((k,) + unit(int(rest)))
+        elif k in ("lx", "lw"):
+            out.append((k, int(rest[0]), int(rest[1])))
+        else:
+            out.append((w,))
+    return out
+
+
+def share(i, g):
+    return SHARE[2 * i + g]
+
+
+def producers(op):
+    k = op[0]
+    if k == "ex":
+        return [("tx",) + op[1:]]
+    if k == "qx":
+        return [("ex",) + op[1:]]
+    if k == "tx":
+        return [("lx", op[1], op[2] // 2), ("gp",)]
+    if k == "tab1":
+        return [("gp",)]
+    if k == "warm":
+        return [("gp",)]
+    if k == "sin":
+        return [("tab1",), ("warm",)]
+    if k == "tab2":
+        return [("sin",)]
+    if k in ("iv", "is"):
+        kind, a = TILES[op[1]]
+        return [("lw", c, op[2]) for c in ([a] if kind == "qk" else [2 * a, 2 * a + 1])]
+    if k == "qw":
+        r = []
+        if share(op[1], op[2]) < 512:
+            r.append(("iv",) + op[1:])
+        if share(op[1], op[2]) > 0:
+            r.append(("is",) + op[1:])
+        return r
+    if k == "mm":
+        return [("qx", op[2], op[3]), ("qw", op[1], 0), ("qw", op[1], 1)]
+    if k == "rm":
+        return [("mm",) + op[1:], ("tab2",)]
+    if k == "cp":
+        return [("mm",) + op[1:4]] + ([("rm",) + op[1:4]] if TILES[op[1]][0] == "qk" else [])
+    if k == "ra":
+        return [("rm", op[1], op[2], m) for m in range(4)]
+    if k == "st":
+        return [("CP", op[1], op[2], m) for m in range(4)] + ([("ra", op[1], op[2])] if TILES[op[1]][0] == "qk" else [])
+    return []
+
+
+def merge(lists):
+    extra = {}
+    pe = lists[0]
+    for n in range(8, len(pe)):
+        o = pe[n - 8]
+        if o[0] == "tx":
+            extra[pe[n]] = [("ex",) + o[1:]]
+        else:
+            extra[pe[n]] = [("CP",) + o[1:]] + ([("rm",) + o[1:]] if TILES[o[1]][0] == "qk" else [])
+    exs = [o for o in lists[2] if o[0] == "ex"]
+    for n in range(4, len(exs)):
+        extra[exs[n]] = [("qx",) + exs[n - 4][1:]]
+    for i in range(len(TILES)):
+        for g in range(G):
+            n = 2 * i + g
+            if n >= NWG:
+                for k in ("iv", "is"):
+                    extra[(k, i, g)] = [("qw", (n - NWG) // 2, (n - NWG) % 2)]
+    idx = [0 for q in lists]
+    done = set()
+    out = []
+    total = sum([len(q) for q in lists])
+    while len(out) < total:
+        progress = False
+        for e in range(len(lists)):
+            while idx[e] < len(lists[e]):
+                op = lists[e][idx[e]]
+                if not all([p in done for p in producers(op) + extra.get(op, [])]):
+                    break
+                out.append(op)
+                done.add(op)
+                if op[0] == "cp":
+                    done.add(("CP",) + op[1:4])
+                idx[e] += 1
+                progress = True
+        if not progress:
+            raise ValueError("the queues' orders cannot be merged: " + str([lists[e][idx[e]] for e in range(len(lists)) if idx[e] < len(lists[e])]))
+    return out
 
 
 def tile_gptneoxjapaneseattention_pa_kernel(tc, hidden_states, w_qkv, out_0, out_1, out_2):
@@ -29,158 +168,185 @@ def tile_gptneoxjapaneseattention_pa_kernel(tc, hidden_states, w_qkv, out_0, out
     with ExitStack() as ctx:
         keep = ctx.enter_context(tc.tile_pool(name="keep", bufs=1))
         xg_pool = ctx.enter_context(tc.tile_pool(name="xg", bufs=4))
-        wg_pool = ctx.enter_context(tc.tile_pool(name="wg", bufs=4))
-        o_pool = ctx.enter_context(tc.tile_pool(name="o", bufs=10))
+        wg_pool = ctx.enter_context(tc.tile_pool(name="wg", bufs=1))
+        o_pool = ctx.enter_context(tc.tile_pool(name="o", bufs=9))
         bt_pool = ctx.enter_context(tc.tile_pool(name="bt", bufs=3))
         psum = ctx.enter_context(tc.psum_pool(name="psum", bufs=8))
+        ctx.enter_context(tc.manual_schedule())
 
         zero = keep.tile([P, 1], F32, name="zero")
-        nc.gpsimd.memset(zero[:], 0.0)
         warm = keep.tile([P, 1], F32, name="warm")
-        nc.scalar.activation(out=warm[:], in_=zero[:], func=ACT.Sin)
-
+        ident = keep.tile([P, P], F32, name="ident")
         xraw = [keep.tile([P, MT, D], BF16, name="xraw%d" % b) for b in range(B)]
         wraw = [[keep.tile([P, 4, CH], BF16, name="wraw%d_%d" % (a, g)) for g in range(G)] for a in range(4)]
-
-        def load_x(b):
-            src = hidden_states[b].rearrange("(p m) k -> p m k", m=MT)
-            for h in range(2):
-                nc.sync.dma_start(out=xraw[b][:, 2 * h : 2 * h + 2, :], in_=src[:, 2 * h : 2 * h + 2, :])
-
-        def load_w(a):
-            for g in range(G):
-                nc.sync.dma_start(
-                    out=wraw[a][g][:],
-                    in_=w_qkv[512 * g : 512 * (g + 1), CH * a : CH * (a + 1)].rearrange("(p j) w -> p j w", j=4),
-                )
-
-        load_x(0)
-        load_w(0)
-        load_x(1)
-        load_w(1)
-        load_w(2)
-        load_w(3)
-
-        ident = keep.tile([P, P], F32, name="ident")
-        make_identity(nc, ident[:])
-
         W = MT * ROT
         pos = keep.tile([P, W], F32, name="pos")
-        nc.gpsimd.iota(pos[:], pattern=[[1, MT], [0, ROT]], base=0, channel_multiplier=MT,
-                       allow_small_or_imprecise_dtypes=True)
         turns = keep.tile([P, W], F32, name="turns")
-        pos_v = pos[:].rearrange("p (a j) -> p a j", j=HALF)
-        turns_v = turns[:].rearrange("p (a j) -> p a j", j=HALF)
-        for j in range(HALF):
-            c_j = 1.0 / (BASE ** (2.0 * j / ROT)) / (2.0 * math.pi)
-            nc.vector.tensor_scalar(out=turns_v[:, :, j : j + 1], in0=pos_v[:, :, j : j + 1],
-                                    scalar1=c_j, scalar2=None, op0=ALU.mult)
         whole_i = keep.tile([P, W], I32, name="whole_i")
-        nc.vector.tensor_copy(out=whole_i[:], in_=turns[:])
         whole_f = keep.tile([P, W], F32, name="whole_f")
-        nc.vector.tensor_copy(out=whole_f[:], in_=whole_i[:])
         frac = keep.tile([P, W], F32, name="frac")
-        nc.vector.tensor_tensor(out=frac[:], in0=turns[:], in1=whole_f[:], op=ALU.subtract)
         s_half = keep.tile([P, W], F32, name="s_half")
-        nc.scalar.activation(out=s_half[:], in_=frac[:], func=ACT.Sin, scale=math.pi)
         s_quar = keep.tile([P, W], F32, name="s_quar")
-        nc.scalar.activation(out=s_quar[:], in_=frac[:], func=ACT.Sin, scale=math.pi / 2.0)
         sq = keep.tile([P, W], F32, name="sq")
-        nc.vector.tensor_tensor(out=sq[:], in0=s_half[:], in1=s_half[:], op=ALU.mult)
-        cos_t = keep.tile([P, MT, ROT], F32, name="cos_t")
-        nc.vector.tensor_scalar(out=cos_t[:].rearrange("p m r -> p (m r)"), in0=sq[:],
-                                scalar1=-2.0, scalar2=1.0, op0=ALU.mult, op1=ALU.add)
         sq2 = keep.tile([P, W], F32, name="sq2")
-        nc.vector.tensor_tensor(out=sq2[:], in0=s_quar[:], in1=s_quar[:], op=ALU.mult)
         c_half = keep.tile([P, W], F32, name="c_half")
-        nc.vector.tensor_scalar(out=c_half[:], in0=sq2[:], scalar1=-2.0, scalar2=1.0, op0=ALU.mult, op1=ALU.add)
+        cos_t = keep.tile([P, MT, ROT], F32, name="cos_t")
         sin_t = keep.tile([P, MT, ROT], F32, name="sin_t")
-        sh_v = s_half[:].rearrange("p (m h j) -> p m h j", m=MT, h=2)
-        ch_v = c_half[:].rearrange("p (m h j) -> p m h j", m=MT, h=2)
-        st_v = sin_t[:].rearrange("p m (h j) -> p m h j", h=2)
-        for h, sign in ((0, 2.0), (1, -2.0)):
-            nc.vector.scalar_tensor_tensor(out=st_v[:, :, h, :], in0=sh_v[:, :, h, :], scalar=sign,
-                                           in1=ch_v[:, :, h, :], op0=ALU.mult, op1=ALU.mult)
-
         xcodes = [keep.tile([P, MT, G, P], U32, name="xcodes%d" % b, align_bytes=64) for b in range(B)]
         xscales = [keep.tile([P, MT, G, P], U8, name="xscales%d" % b, align_bytes=64) for b in range(B)]
-
-        def prep_x(b):
-            for m in range(MT):
-                words = xraw[b][:, m, :].bitcast(F32)
-                xt = psum.tile([P, G, 2, P], F32, tag="bank", name="xt")
-                for g in range(G):
-                    for u in range(2):
-                        nc.tensor.transpose(xt[:, g, u, :], words[:, 256 * g + u : 256 * (g + 1) : 2], ident[:])
-                xg = xg_pool.tile([P, G, P, 4], BF16, name="xg", align_bytes=64)
-                nc.scalar.copy(out=xg[:].bitcast(F32), in_=xt[:].rearrange("p g u r -> p g r u"))
-                nc.vector.quantize_mx(
-                    out=xcodes[b][:, m].rearrange("p g r -> p (g r)").bitcast(FP8X4),
-                    scales=xscales[b][:, m].rearrange("p g r -> p (g r)"),
-                    in_=xg[:].rearrange("p g r t -> p (g r t)"),
-                )
-
-        tiles = [("qk", 0), ("qk", 1), ("v", 0), ("qk", 2), ("qk", 3), ("v", 1)]
         wcodes = [keep.tile([P, G, 512], U32, name="wcodes%d" % i, align_bytes=64) for i in range(6)]
         wscales = [keep.tile([P, G, 512], U8, name="wscales%d" % i, align_bytes=64) for i in range(6)]
+        xt = {}
+        xgs = {}
+        wgs = {}
+        pss = {}
+        osbs = {}
+        bts = {}
 
-        def interleave(on_vector, dst, src):
-            d = dst.rearrange("p (c i) j -> p c j i", i=4)
-            s = src.rearrange("p j (c i) -> p c j i", i=4)
-            if on_vector:
-                nc.vector.tensor_copy(out=d, in_=s)
-            else:
-                nc.scalar.copy(out=d, in_=s)
+        def gp():
+            nc.gpsimd.memset(zero[:], 0.0)
+            nc.gpsimd.iota(pos[:], pattern=[[1, MT], [0, ROT]], base=0, channel_multiplier=MT,
+                           allow_small_or_imprecise_dtypes=True)
+            make_identity(nc, ident[:])
 
-        def prep_w(i):
-            kind, a = tiles[i]
+        def tab1():
+            pos_v = pos[:].rearrange("p (a j) -> p a j", j=HALF)
+            turns_v = turns[:].rearrange("p (a j) -> p a j", j=HALF)
+            for j in range(HALF):
+                c_j = 1.0 / (BASE ** (2.0 * j / ROT)) / (2.0 * math.pi)
+                nc.vector.tensor_scalar(out=turns_v[:, :, j : j + 1], in0=pos_v[:, :, j : j + 1],
+                                        scalar1=c_j, scalar2=None, op0=ALU.mult)
+            nc.vector.tensor_copy(out=whole_i[:], in_=turns[:])
+            nc.vector.tensor_copy(out=whole_f[:], in_=whole_i[:])
+            nc.vector.tensor_tensor(out=frac[:], in0=turns[:], in1=whole_f[:], op=ALU.subtract)
+
+        def sins():
+            nc.scalar.activation(out=s_half[:], in_=frac[:], func=ACT.Sin, scale=math.pi)
+            nc.scalar.activation(out=s_quar[:], in_=frac[:], func=ACT.Sin, scale=math.pi / 2.0)
+
+        def tab2():
+            nc.vector.tensor_tensor(out=sq[:], in0=s_half[:], in1=s_half[:], op=ALU.mult)
+            nc.vector.tensor_tensor(out=sq2[:], in0=s_quar[:], in1=s_quar[:], op=ALU.mult)
+            nc.vector.tensor_scalar(out=cos_t[:].rearrange("p m r -> p (m r)"), in0=sq[:],
+                                    scalar1=-2.0, scalar2=1.0, op0=ALU.mult, op1=ALU.add)
+            nc.vector.tensor_scalar(out=c_half[:], in0=sq2[:], scalar1=-2.0, scalar2=1.0, op0=ALU.mult, op1=ALU.add)
+            sh_v = s_half[:].rearrange("p (m h j) -> p m h j", m=MT, h=2)
+            ch_v = c_half[:].rearrange("p (m h j) -> p m h j", m=MT, h=2)
+            st_v = sin_t[:].rearrange("p m (h j) -> p m h j", h=2)
+            for h, sign in ((0, 2.0), (1, -2.0)):
+                nc.vector.scalar_tensor_tensor(out=st_v[:, :, h, :], in0=sh_v[:, :, h, :], scalar=sign,
+                                               in1=ch_v[:, :, h, :], op0=ALU.mult, op1=ALU.mult)
+
+        def lx(b, h):
+            src = hidden_states[b].rearrange("(p m) k -> p m k", m=MT)
+            nc.sync.dma_start(out=xraw[b][:, 2 * h : 2 * h + 2, :], in_=src[:, 2 * h : 2 * h + 2, :])
+
+        def lw(a, g):
+            nc.sync.dma_start(
+                out=wraw[a][g][:],
+                in_=w_qkv[512 * g : 512 * (g + 1), CH * a : CH * (a + 1)].rearrange("(p j) w -> p j w", j=4),
+            )
+
+        def tx(b, m):
+            words = xraw[b][:, m, :].bitcast(F32)
+            t = psum.tile([P, G, 2, P], F32, tag="bank", name="xt")
             for g in range(G):
-                wg = wg_pool.tile([P, 512, 4], BF16, name="wg", align_bytes=64)
-                if kind == "qk":
-                    for hh in range(2):
-                        interleave(not (hh == 1 and g == 1), wg[:, 256 * hh : 256 * (hh + 1), :],
-                                   wraw[a][g][:, :, 384 * hh : 384 * hh + 256])
-                else:
-                    for u in range(4):
-                        interleave(u < 2 or (u == 2 and g == 0), wg[:, 128 * u : 128 * (u + 1), :],
-                                   wraw[2 * a + u // 2][g][:, :, 384 * (u % 2) + 256 : 384 * (u % 2) + 384])
-                nc.vector.quantize_mx(
-                    out=wcodes[i][:, g, :].bitcast(FP8X4),
-                    scales=wscales[i][:, g, :],
-                    in_=wg[:].rearrange("p w j -> p (w j)"),
-                )
+                for u in range(2):
+                    nc.tensor.transpose(t[:, g, u, :], words[:, 256 * g + u : 256 * (g + 1) : 2], ident[:])
+            xt[(b, m)] = t
 
-        def product(i, b):
-            kind, a = tiles[i]
-            osb = o_pool.tile([P, 4, MT, HS], F32, name="osb")
-            bt = None
+        def ex(b, m):
+            xg = xg_pool.tile([P, G, P, 4], BF16, name="xg", align_bytes=64)
+            nc.scalar.copy(out=xg[:].bitcast(F32), in_=xt[(b, m)][:].rearrange("p g u r -> p g r u"))
+            xgs[(b, m)] = xg
+
+        def qx(b, m):
+            nc.vector.quantize_mx(
+                out=xcodes[b][:, m].rearrange("p g r -> p (g r)").bitcast(FP8X4),
+                scales=xscales[b][:, m].rearrange("p g r -> p (g r)"),
+                in_=xgs[(b, m)][:].rearrange("p g r t -> p (g r t)"),
+            )
+
+        def pieces(i):
+            kind, a = TILES[i]
             if kind == "qk":
-                bt = bt_pool.tile([P, 4, MT, ROT], F32, name="bt")
-            for m in range(MT):
-                ps = psum.tile([P, 4, HS], F32, tag="bank", name="ps")
-                for g in range(G):
-                    nc.tensor.matmul_mx(
-                        out=ps[:].rearrange("p u f -> p (u f)"),
-                        lhsT=xcodes[b][:, m, g, :].bitcast(FP8X4),
-                        lhsT_scale=xscales[b][:, m, g, :],
-                        rhs=wcodes[i][:, g, :].bitcast(FP8X4),
-                        rhs_scale=wscales[i][:, g, :],
-                        start=(g == 0),
-                        stop=(g == G - 1),
-                    )
-                if kind == "qk":
-                    nc.vector.tensor_tensor(out=osb[:, :, m, 0:ROT], in0=ps[:, :, 0:ROT],
-                                            in1=cos_t[:, m : m + 1, :].to_broadcast([P, 4, ROT]), op=ALU.mult)
-                    nc.vector.tensor_tensor(out=bt[:, :, m, :], in0=ps[:, :, 0:ROT],
-                                            in1=sin_t[:, m : m + 1, :].to_broadcast([P, 4, ROT]), op=ALU.mult)
-                    nc.scalar.copy(out=osb[:, :, m, ROT:HS], in_=ps[:, :, ROT:HS])
+                return [(256 * hh, 256, a, 384 * hh) for hh in range(2)]
+            return [(128 * u, 128, 2 * a + u // 2, 384 * (u % 2) + 256) for u in range(4)]
+
+        def interleave(i, g, on_vector):
+            if (i, g) not in wgs:
+                wgs[(i, g)] = wg_pool.tile([P, 512, 4], BF16, name="wg%d" % ((2 * i + g) % NWG), align_bytes=64)
+            wg = wgs[(i, g)]
+            cut = 512 - share(i, g)
+            for d0, wd, a, s0 in pieces(i):
+                lo = max(d0, 0 if on_vector else cut)
+                hi = min(d0 + wd, cut if on_vector else 512)
+                if hi <= lo:
+                    continue
+                dst = wg[:, lo:hi, :].rearrange("p (c i) j -> p c j i", i=4)
+                src = wraw[a][g][:, :, s0 + lo - d0 : s0 + hi - d0].rearrange("p j (c i) -> p c j i", i=4)
+                if on_vector:
+                    nc.vector.tensor_copy(out=dst, in_=src)
                 else:
-                    nc.scalar.copy(out=osb[:, :, m, :], in_=ps[:])
+                    nc.scalar.copy(out=dst, in_=src)
+
+        def qw(i, g):
+            nc.vector.quantize_mx(
+                out=wcodes[i][:, g, :].bitcast(FP8X4),
+                scales=wscales[i][:, g, :],
+                in_=wgs[(i, g)][:].rearrange("p w j -> p (w j)"),
+            )
+
+        def mm(i, b, m):
+            ps = psum.tile([P, 4, HS], F32, tag="bank", name="ps")
+            for g in range(G):
+                nc.tensor.matmul_mx(
+                    out=ps[:].rearrange("p u f -> p (u f)"),
+                    lhsT=xcodes[b][:, m, g, :].bitcast(FP8X4),
+                    lhsT_scale=xscales[b][:, m, g, :],
+                    rhs=wcodes[i][:, g, :].bitcast(FP8X4),
+                    rhs_scale=wscales[i][:, g, :],
+                    start=(g == 0),
+                    stop=(g == G - 1),
+                )
+            pss[(i, b, m)] = ps
+
+        def osb_of(i, b):
+            if (i, b) not in osbs:
+                osbs[(i, b)] = o_pool.tile([P, 4, MT, HS], F32, name="osb")
+            return osbs[(i, b)]
+
+        def rm(i, b, m):
+            osb = osb_of(i, b)
+            if (i, b) not in bts:
+                bts[(i, b)] = bt_pool.tile([P, 4, MT, ROT], F32, name="bt")
+            ps = pss[(i, b, m)]
+            nc.vector.tensor_tensor(out=osb[:, :, m, 0:ROT], in0=ps[:, :, 0:ROT],
+                                    in1=cos_t[:, m : m + 1, :].to_broadcast([P, 4, ROT]), op=ALU.mult)
+            nc.vector.tensor_tensor(out=bts[(i, b)][:, :, m, :], in0=ps[:, :, 0:ROT],
+                                    in1=sin_t[:, m : m + 1, :].to_broadcast([P, 4, ROT]), op=ALU.mult)
+
+        def cp(i, b, m, eng):
+            osb = osb_of(i, b)
+            ps = pss[(i, b, m)]
+            lo = ROT if TILES[i][0] == "qk" else 0
+            if eng == "S":
+                nc.scalar.copy(out=osb[:, :, m, lo:HS], in_=ps[:, :, lo:HS])
+            else:
+                nc.vector.tensor_copy(out=osb[:, :, m, lo:HS], in_=ps[:, :, lo:HS])
+
+        def ra(i, b):
+            osb = osbs[(i, b)]
+            bt = bts[(i, b)]
+            nc.vector.tensor_tensor(out=osb[:, :, :, 0:HALF], in0=osb[:, :, :, 0:HALF],
+                                    in1=bt[:, :, :, HALF:ROT], op=ALU.add)
+            nc.vector.tensor_tensor(out=osb[:, :, :, HALF:ROT], in0=osb[:, :, :, HALF:ROT],
+                                    in1=bt[:, :, :, 0:HALF], op=ALU.add)
+
+        def st(i, b):
+            kind, a = TILES[i]
+            osb = osbs[(i, b)]
             if kind == "qk":
-                nc.vector.tensor_tensor(out=osb[:, :, :, 0:HALF], in0=osb[:, :, :, 0:HALF],
-                                        in1=bt[:, :, :, HALF:ROT], op=ALU.add)
-                nc.vector.tensor_tensor(out=osb[:, :, :, HALF:ROT], in0=osb[:, :, :, HALF:ROT],
-                                        in1=bt[:, :, :, 0:HALF], op=ALU.add)
                 by_kind = osb[:].rearrange("p (hh s) m f -> p s hh (m f)", s=2)
                 for s, dst in ((0, out_0), (1, out_1)):
                     nc.sync.dma_start(out=dst[b, 2 * a : 2 * a + 2].rearrange("h (p m) f -> p h (m f)", m=MT),
@@ -189,12 +355,43 @@ def tile_gptneoxjapaneseattention_pa_kernel(tc, hidden_states, w_qkv, out_0, out
                 nc.sync.dma_start(out=out_2[b, 4 * a : 4 * a + 4].rearrange("h (p m) f -> p h (m f)", m=MT),
                                   in_=osb[:].rearrange("p u m f -> p u (m f)"))
 
-        prep_x(0)
-        prep_w(0)
-        for i in range(6):
-            if i + 1 < 6:
-                prep_w(i + 1)
-            product(i, 0)
-            if i == 0:
-                prep_x(1)
-            product(i, 1)
+        for op in merge([parse(Q_PE), parse(Q_V), parse(Q_S), parse(Q_SP), [("gp",)]]):
+            k = op[0]
+            if k == "gp":
+                gp()
+            elif k == "warm":
+                nc.scalar.activation(out=warm[:], in_=zero[:], func=ACT.Sin)
+            elif k == "tab1":
+                tab1()
+            elif k == "sin":
+                sins()
+            elif k == "tab2":
+                tab2()
+            elif k == "lx":
+                lx(op[1], op[2])
+            elif k == "lw":
+                lw(op[1], op[2])
+            elif k == "tx":
+                tx(op[1], op[2])
+            elif k == "ex":
+                ex(op[1], op[2])
+            elif k == "qx":
+                qx(op[1], op[2])
+            elif k == "iv":
+                interleave(op[1], op[2], True)
+            elif k == "is":
+                interleave(op[1], op[2], False)
+            elif k == "qw":
+                qw(op[1], op[2])
+            elif k == "mm":
+                mm(op[1], op[2], op[3])
+            elif k == "rm":
+                rm(op[1], op[2], op[3])
+            elif k == "cp":
+                cp(op[1], op[2], op[3], op[4])
+            elif k == "ra":
+                ra(op[1], op[2])
+            elif k == "st":
+                st(op[1], op[2])
+            else:
+                raise ValueError(k)

@@ -24,21 +24,18 @@ MT = 4
 CH = 768
 NWG = 6
 
-TILES = [("qk", 0), ("qk", 1), ("v", 0), ("qk", 2), ("v", 1), ("qk", 3)]
-SHARE = [192, 192, 128, 128, 256, 256, 256, 256, 128, 128, 256, 256]
+TILES = [("qk", 0), ("v", 0), ("qk", 1), ("v", 1), ("qk", 2), ("qk", 3)]
+SHARE = [(320, 512), (320, 512), (0, 256), (0, 256), (256, 512), (256, 512), (512, 512), (512, 512), (256, 512), (256, 512), (512, 512), (512, 512)]
 Q_PE = """tx0 mm0 tx1 mm1 mm2 mm3 mm4 mm5 mm6 mm7 mm8 mm9 mm10 mm11"""
 Q_V = """tab1 tab2 iv-2 qx0.01 iv-1 qw-2 qw-1 qx0.23
  rm0 iv0 ra0 qx1.01 iv1 qx1.23 qw0 qw1
- rm1 iv2 ra1 iv3 qw2
- rm2 qw3 ra2 iv4
- rm3 iv5 ra3 qw4 qw5
- iv6 iv7 qw6 qw7
- rm6 iv8 ra6 iv9
- rm7 qw8 ra7 qw9
- cv8.13 cv9.13
- rm10 ra10 rm11 ra11"""
-Q_S = """warm sin ex0.01 is-2 is-1 ex0.23
- cp0 ex1 is0 is1 is2 is3 cp1 cp2 is4 is5 cp3 cp4 is6 is7 cp5 is8 is9 cp6 cp7 cp8.02 cp9.02 cp10 cp11"""
+ rm1 iv2 ra1 iv3 qw2 iv4 qw3 iv5 qw4 qw5
+ rm4 iv6 ra4 iv7
+ rm5 qw6 ra5 qw7
+ iv8 iv9 qw8 qw9
+ rm8 ra8 rm9 ra9 rm10 ra10 rm11 ra11"""
+Q_S = """warm sin ex0.01 is-2 is-1 is0 ex0.23 is1
+ cp0 ex1 is2 is3 cp1 cp2 cp3 is6 cp4 is7 cp5 cp6 cp7 cp8 cp9 cp10 cp11"""
 Q_SP = """lx00 lw00 lw01 lx01 lx10 lx11 lw10 lw11 lw20 lw21 lw30 lw31 st0 st1 st2 st3 st4 st5 st6 st7 st8 st9 st10 st11"""
 
 
@@ -80,8 +77,23 @@ def parse(txt):
     return out
 
 
-def share(i, g):
-    return SHARE[2 * i + g]
+def pieces(i):
+    kind, a = TILES[i]
+    if kind == "qk":
+        return [(256 * hh, 256, a, 384 * hh) for hh in range(2)]
+    return [(128 * u, 128, 2 * a + u // 2, 384 * (u % 2) + 256) for u in range(4)]
+
+
+def cut_pieces(i, g, on_vector):
+    lo, hi = SHARE[2 * i + g]
+    out = []
+    for r0, r1 in ([(0, lo), (hi, 512)] if on_vector else [(lo, hi)]):
+        for d0, wd, a, s0 in pieces(i):
+            x0 = max(d0, r0)
+            x1 = min(d0 + wd, r1)
+            if x1 > x0:
+                out.append((x0, x1 - x0, a, s0 + x0 - d0))
+    return out
 
 
 def producers(op):
@@ -101,15 +113,9 @@ def producers(op):
     if k == "tab2":
         return [("sin",)]
     if k in ("iv", "is"):
-        kind, a = TILES[op[1]]
-        return [("lw", c, op[2]) for c in ([a] if kind == "qk" else [2 * a, 2 * a + 1])]
+        return [("lw", a, op[2]) for d0, wd, a, s0 in cut_pieces(op[1], op[2], k == "iv")]
     if k == "qw":
-        r = []
-        if share(op[1], op[2]) < 512:
-            r.append(("iv",) + op[1:])
-        if share(op[1], op[2]) > 0:
-            r.append(("is",) + op[1:])
-        return r
+        return [(e,) + op[1:] for e in ("iv", "is") if cut_pieces(op[1], op[2], e == "iv")]
     if k == "mm":
         return [("qx", op[2], op[3]), ("qw", op[1], 0), ("qw", op[1], 1)]
     if k == "rm":
@@ -267,24 +273,13 @@ def tile_gptneoxjapaneseattention_pa_kernel(tc, hidden_states, w_qkv, out_0, out
                 in_=xgs[(b, m)][:].rearrange("p g r t -> p (g r t)"),
             )
 
-        def pieces(i):
-            kind, a = TILES[i]
-            if kind == "qk":
-                return [(256 * hh, 256, a, 384 * hh) for hh in range(2)]
-            return [(128 * u, 128, 2 * a + u // 2, 384 * (u % 2) + 256) for u in range(4)]
-
         def interleave(i, g, on_vector):
             if (i, g) not in wgs:
                 wgs[(i, g)] = wg_pool.tile([P, 512, 4], BF16, name="wg%d" % ((2 * i + g) % NWG), align_bytes=64)
             wg = wgs[(i, g)]
-            cut = 512 - share(i, g)
-            for d0, wd, a, s0 in pieces(i):
-                lo = max(d0, 0 if on_vector else cut)
-                hi = min(d0 + wd, cut if on_vector else 512)
-                if hi <= lo:
-                    continue
-                dst = wg[:, lo:hi, :].rearrange("p (c i) j -> p c j i", i=4)
-                src = wraw[a][g][:, :, s0 + lo - d0 : s0 + hi - d0].rearrange("p j (c i) -> p c j i", i=4)
+            for d0, wd, a, s0 in cut_pieces(i, g, on_vector):
+                dst = wg[:, d0 : d0 + wd, :].rearrange("p (c i) j -> p c j i", i=4)
+                src = wraw[a][g][:, :, s0 : s0 + wd].rearrange("p j (c i) -> p c j i", i=4)
                 if on_vector:
                     nc.vector.tensor_copy(out=dst, in_=src)
                 else:

@@ -21,7 +21,8 @@ ACT = mybir.ActivationFunctionType
 P = 128
 G = 2
 MT = 4
-CH = 768
+CHUNKS = [(0, 768), (768, 768), (1536, 1536)]
+KINDS = {"q": 0, "k": 1, "v": 2}
 NWG = 6
 
 TILES = [("qk", 0), ("v", 0), ("qk", 1), ("v", 1), ("qk", 2), ("qk", 3)]
@@ -36,7 +37,7 @@ Q_V = """tab1 tab2 iv-2 qx0.01 iv-1 qw-2 qw-1 qx0.23
  rm8 ra8 rm9 ra9 rm10 ra10 rm11 ra11"""
 Q_S = """warm sin ex0.01 is-2 is-1 is0 ex0.23 is1
  cp0 ex1 is2 is3 cp1 cp2 cp3 is6 cp4 is7 cp5 cp6 cp7 cp8 cp9 cp10 cp11"""
-Q_SP = """lx00 lw00 lw01 lx01 lx10 lx11 lw10 lw11 lw20 lw21 lw30 lw31 st0 st1 st2 st3 st4 st5 st6 st7 st8 st9 st10 st11"""
+Q_SP = """lx00 lw00 lw01 lx01 lx12 lw10 lw11 lw20 lw21 st0 st1 st2 st3 st4 st5 st6 st7 st8 st9 st10 st11"""
 
 
 def unit(u):
@@ -77,11 +78,25 @@ def parse(txt):
     return out
 
 
+def rotated(i):
+    return TILES[i][0] != "v"
+
+
 def pieces(i):
     kind, a = TILES[i]
     if kind == "qk":
-        return [(256 * hh, 256, a, 384 * hh) for hh in range(2)]
-    return [(128 * u, 128, 2 * a + u // 2, 384 * (u % 2) + 256) for u in range(4)]
+        cols = [384 * (2 * a + u // 2) + 128 * (u % 2) for u in range(4)]
+    else:
+        cols = [384 * (4 * a + u) + 128 * KINDS[kind] for u in range(4)]
+    out = []
+    for u in range(4):
+        c = [n for n in range(len(CHUNKS)) if CHUNKS[n][0] <= cols[u] < CHUNKS[n][0] + CHUNKS[n][1]][0]
+        s0 = cols[u] - CHUNKS[c][0]
+        if out and out[-1][2] == c and out[-1][3] + out[-1][1] == s0:
+            out[-1] = (out[-1][0], out[-1][1] + 128, c, out[-1][3])
+        else:
+            out.append((128 * u, 128, c, s0))
+    return out
 
 
 def cut_pieces(i, g, on_vector):
@@ -103,7 +118,7 @@ def producers(op):
     if k == "qx":
         return [("ex",) + op[1:]]
     if k == "tx":
-        return [("lx", op[1], op[2] // 2), ("gp",)]
+        return [("LX", op[1], op[2] // 2), ("gp",)]
     if k == "tab1":
         return [("gp",)]
     if k == "warm":
@@ -121,11 +136,11 @@ def producers(op):
     if k == "rm":
         return [("mm",) + op[1:], ("tab2",)]
     if k == "cp":
-        return [("mm",) + op[1:4]] + ([("rm",) + op[1:4]] if TILES[op[1]][0] == "qk" else [])
+        return [("mm",) + op[1:4]] + ([("rm",) + op[1:4]] if rotated(op[1]) else [])
     if k == "ra":
         return [("rm", op[1], op[2], m) for m in range(4)]
     if k == "st":
-        return [("CP", op[1], op[2], m) for m in range(4)] + ([("ra", op[1], op[2])] if TILES[op[1]][0] == "qk" else [])
+        return [("CP", op[1], op[2], m) for m in range(4)] + ([("ra", op[1], op[2])] if rotated(op[1]) else [])
     return []
 
 
@@ -137,7 +152,7 @@ def merge(lists):
         if o[0] == "tx":
             extra[pe[n]] = [("ex",) + o[1:]]
         else:
-            extra[pe[n]] = [("CP",) + o[1:]] + ([("rm",) + o[1:]] if TILES[o[1]][0] == "qk" else [])
+            extra[pe[n]] = [("CP",) + o[1:]] + ([("rm",) + o[1:]] if rotated(o[1]) else [])
     exs = [o for o in lists[2] if o[0] == "ex"]
     for n in range(4, len(exs)):
         extra[exs[n]] = [("qx",) + exs[n - 4][1:]]
@@ -162,6 +177,9 @@ def merge(lists):
                 done.add(op)
                 if op[0] == "cp":
                     done.add(("CP",) + op[1:4])
+                if op[0] == "lx":
+                    for h in ([0, 1] if op[2] == 2 else [op[2]]):
+                        done.add(("LX", op[1], h))
                 idx[e] += 1
                 progress = True
         if not progress:
@@ -184,7 +202,7 @@ def tile_gptneoxjapaneseattention_pa_kernel(tc, hidden_states, w_qkv, out_0, out
         warm = keep.tile([P, 1], F32, name="warm")
         ident = keep.tile([P, P], F32, name="ident")
         xraw = [keep.tile([P, MT, D], BF16, name="xraw%d" % b) for b in range(B)]
-        wraw = [[keep.tile([P, 4, CH], BF16, name="wraw%d_%d" % (a, g)) for g in range(G)] for a in range(4)]
+        wraw = [[keep.tile([P, 4, CHUNKS[a][1]], BF16, name="wraw%d_%d" % (a, g)) for g in range(G)] for a in range(len(CHUNKS))]
         W = MT * ROT
         pos = keep.tile([P, W], F32, name="pos")
         turns = keep.tile([P, W], F32, name="turns")
@@ -245,12 +263,15 @@ def tile_gptneoxjapaneseattention_pa_kernel(tc, hidden_states, w_qkv, out_0, out
 
         def lx(b, h):
             src = hidden_states[b].rearrange("(p m) k -> p m k", m=MT)
-            nc.sync.dma_start(out=xraw[b][:, 2 * h : 2 * h + 2, :], in_=src[:, 2 * h : 2 * h + 2, :])
+            if h == 2:
+                nc.sync.dma_start(out=xraw[b][:], in_=src)
+            else:
+                nc.sync.dma_start(out=xraw[b][:, 2 * h : 2 * h + 2, :], in_=src[:, 2 * h : 2 * h + 2, :])
 
         def lw(a, g):
             nc.sync.dma_start(
                 out=wraw[a][g][:],
-                in_=w_qkv[512 * g : 512 * (g + 1), CH * a : CH * (a + 1)].rearrange("(p j) w -> p j w", j=4),
+                in_=w_qkv[512 * g : 512 * (g + 1), CHUNKS[a][0] : CHUNKS[a][0] + CHUNKS[a][1]].rearrange("(p j) w -> p j w", j=4),
             )
 
         def tx(b, m):
@@ -324,7 +345,7 @@ def tile_gptneoxjapaneseattention_pa_kernel(tc, hidden_states, w_qkv, out_0, out
         def cp(i, b, m, eng):
             osb = osb_of(i, b)
             ps = pss[(i, b, m)]
-            lo = ROT if TILES[i][0] == "qk" else 0
+            lo = ROT if rotated(i) else 0
             if eng == "S":
                 nc.scalar.copy(out=osb[:, :, m, lo:HS], in_=ps[:, :, lo:HS])
             else:
@@ -347,7 +368,8 @@ def tile_gptneoxjapaneseattention_pa_kernel(tc, hidden_states, w_qkv, out_0, out
                     nc.sync.dma_start(out=dst[b, 2 * a : 2 * a + 2].rearrange("h (p m) f -> p h (m f)", m=MT),
                                       in_=by_kind[:, s])
             else:
-                nc.sync.dma_start(out=out_2[b, 4 * a : 4 * a + 4].rearrange("h (p m) f -> p h (m f)", m=MT),
+                dst = (out_0, out_1, out_2)[KINDS[kind]]
+                nc.sync.dma_start(out=dst[b, 4 * a : 4 * a + 4].rearrange("h (p m) f -> p h (m f)", m=MT),
                                   in_=osb[:].rearrange("p u m f -> p u (m f)"))
 
         for op in merge([parse(Q_PE), parse(Q_V), parse(Q_S), parse(Q_SP), [("gp",)]]):

@@ -34,7 +34,7 @@ Q_V = """tab1 tab2 iv-2 qx0.01 iv-1 qw-2 qw-1 qx0.23
  rm4 iv6 ra4 iv7
  rm5 qw6 ra5 qw7
  iv8 iv9 qw8 qw9
- rm8 ra8 rm9 ra9 rm10 ra10 rm11 ra11"""
+ rm8 rm9.01 ra8 rm9.23 rm10.01 ra9 rm10.23 rm11.01 ra10 rm11.23 ra11"""
 Q_S = """warm sin ex0.01 is-2 is-1 is0 ex0.23 is1
  cp0 ex1 is2 is3 cp1 cp2 cp3 is6 cp4 is7 cp5 cp6 cp7 cp8 cp9 cp10 cp11"""
 Q_SP = """lx00 lw00 lw01 lx01 lx12 lw10 lw11 lw20 lw21 st0 st1 st2 st3 st4 st5 st6 st7 st8 st9 st10 st11"""
@@ -62,7 +62,7 @@ def parse(txt):
                     out.append(("cp", p // 2, p % 2, m, "V"))
                 else:
                     out.append((k, p // 2, p % 2, m))
-        elif k in ("ra", "st"):
+        elif k in ("ra", "st", "sa", "sb"):
             out.append((k, int(rest) // 2, int(rest) % 2))
         elif k in ("tx", "ex", "qx"):
             ms = list(range(4))
@@ -139,7 +139,7 @@ def producers(op):
         return [("mm",) + op[1:4]] + ([("rm",) + op[1:4]] if rotated(op[1]) else [])
     if k == "ra":
         return [("rm", op[1], op[2], m) for m in range(4)]
-    if k == "st":
+    if k in ("st", "sa", "sb"):
         return [("CP", op[1], op[2], m) for m in range(4)] + ([("ra", op[1], op[2])] if rotated(op[1]) else [])
     return []
 
@@ -359,18 +359,23 @@ def tile_gptneoxjapaneseattention_pa_kernel(tc, hidden_states, w_qkv, out_0, out
             nc.vector.tensor_tensor(out=osb[:, :, :, HALF:ROT], in0=osb[:, :, :, HALF:ROT],
                                     in1=bt[:, :, :, 0:HALF], op=ALU.add)
 
-        def st(i, b):
+        def st(i, b, parts, queue):
             kind, a = TILES[i]
             osb = osbs[(i, b)]
             if kind == "qk":
                 by_kind = osb[:].rearrange("p (hh s) m f -> p s hh (m f)", s=2)
-                for s, dst in ((0, out_0), (1, out_1)):
-                    nc.sync.dma_start(out=dst[b, 2 * a : 2 * a + 2].rearrange("h (p m) f -> p h (m f)", m=MT),
-                                      in_=by_kind[:, s])
+                for s in parts:
+                    queue.dma_start(out=(out_0, out_1)[s][b, 2 * a : 2 * a + 2].rearrange("h (p m) f -> p h (m f)", m=MT),
+                                    in_=by_kind[:, s])
+            elif len(parts) == 2:
+                dst = (out_0, out_1, out_2)[KINDS[kind]]
+                queue.dma_start(out=dst[b, 4 * a : 4 * a + 4].rearrange("h (p m) f -> p h (m f)", m=MT),
+                                in_=osb[:].rearrange("p u m f -> p u (m f)"))
             else:
                 dst = (out_0, out_1, out_2)[KINDS[kind]]
-                nc.sync.dma_start(out=dst[b, 4 * a : 4 * a + 4].rearrange("h (p m) f -> p h (m f)", m=MT),
-                                  in_=osb[:].rearrange("p u m f -> p u (m f)"))
+                h0 = 2 * parts[0]
+                queue.dma_start(out=dst[b, 4 * a + h0 : 4 * a + h0 + 2].rearrange("h (p m) f -> p h (m f)", m=MT),
+                                in_=osb[:, h0 : h0 + 2].rearrange("p u m f -> p u (m f)"))
 
         for op in merge([parse(Q_PE), parse(Q_V), parse(Q_S), parse(Q_SP), [("gp",)]]):
             k = op[0]
@@ -409,6 +414,10 @@ def tile_gptneoxjapaneseattention_pa_kernel(tc, hidden_states, w_qkv, out_0, out
             elif k == "ra":
                 ra(op[1], op[2])
             elif k == "st":
-                st(op[1], op[2])
+                st(op[1], op[2], (0, 1), nc.sync)
+            elif k == "sa":
+                st(op[1], op[2], (0,), nc.sync)
+            elif k == "sb":
+                st(op[1], op[2], (1,), nc.scalar)
             else:
                 raise ValueError(k)

import math
from contextlib import ExitStack

import concourse.mybir as mybir
from concourse.masks import make_identity

B, S, D, NH, HS, ROT = 2, 512, 1024, 8, 128, 32
HALF = ROT // 2
BASE = 10000.0
FLOPS = 2 * B * S * D * 3 * NH * HS

F32 = mybir.dt.float32
BF16 = mybir.dt.bfloat16
I32 = mybir.dt.int32
U32 = mybir.dt.uint32
U8 = mybir.dt.uint8
FP8X4 = mybir.dt.float8_e5m2_x4
ALU = mybir.AluOpType
ACT = mybir.ActivationFunctionType

P = 128
G = 2
MT = 4
CHUNKS = [(0, 768), (768, 768), (1536, 1536)]
KINDS = {"q": 0, "k": 1, "v": 2}
NWG = 6

TILES = [("qk", 0), ("v", 0), ("qk", 1), ("v", 1), ("qk", 2), ("qk", 3)]
SHARE = [(320, 512), (320, 512), (0, 256), (0, 256), (256, 512), (256, 512), (512, 512), (512, 512), (256, 512), (256, 512), (512, 512), (512, 512)]
Q_PE = """tx0 mm0 tx1 mm1 mm2 mm3 mm4 mm5 mm6 mm7 mm8 mm9 mm10 mm11"""
Q_V = """tab1 tab2 iv-2 qx0.01 iv-1 qw-2 qw-1 qx0.23
 rm0 iv0 ra0 qx1.01 iv1 qx1.23 qw0 qw1
 rm1 iv2 ra1 iv3 qw2 iv4 qw3 iv5 qw4 qw5
 rm4 iv6 ra4 iv7
 rm5 qw6 ra5 qw7
 iv8 iv9 qw8 qw9
 rm8 rm9.01 ra8 rm9.23 rm10.01 ra9 rm10.23 rm11.01 ra10 rm11.23 ra11"""
Q_S = """warm sin ex0.01 is-2 is-1 is0 ex0.23 is1
 cp0 ex1 is2 is3 cp1 cp2 cp3 is6 cp4 is7 cp5 cp6 cp7 cp8 cp9 cp10 cp11"""
Q_SP = """lx00 lw00 lw01 lx01 lx12 lw10 lw11 lw20 lw21 st0 st1 st2 st3 st4 st5 st6 st7 st8 st9 st10 st11"""


def unit(u):
    return (1 + u // 2, u % 2) if u >= 0 else (0, u + 2)


def parse(txt):
    out = []
    for w in txt.split():
        k = w[:2]
        rest = w[2:]
        if k in ("rm", "cp", "mm", "cv"):
            ms = list(range(4))
            if "." in rest:
                ms = [int(c) for c in rest.split(".")[1]]
                rest = rest.split(".")[0]
            p = int(rest)
            for m in ms:
                if k == "cp":
                    out.append(("cp", p // 2, p % 2, m, "S"))
                elif k == "cv":
                    out.append(("cp", p // 2, p % 2, m, "V"))
                else:
                    out.append((k, p // 2, p % 2, m))
        elif k in ("ra", "st", "sa", "sb"):
            out.append((k, int(rest) // 2, int(rest) % 2))
        elif k in ("tx", "ex", "qx"):
            ms = list(range(4))
            if "." in rest:
                ms = [int(c) for c in rest.split(".")[1]]
            out.extend([(k, int(rest[0]), m) for m in ms])
        elif k in ("iv", "is", "qw"):
            out.append((k,) + unit(int(rest)))
        elif k in ("lx", "lw"):
            out.append((k, int(rest[0]), int(rest[1])))
        else:
            out.append((w,))
    return out


def rotated(i):
    return TILES[i][0] != "v"


def pieces(i):
    kind, a = TILES[i]
    if kind == "qk":
        cols = [384 * (2 * a + u // 2) + 128 * (u % 2) for u in range(4)]
    else:
        cols = [384 * (4 * a + u) + 128 * KINDS[kind] for u in range(4)]
    out = []
    for u in range(4):
        c = [n for n in range(len(CHUNKS)) if CHUNKS[n][0] <= cols[u] < CHUNKS[n][0] + CHUNKS[n][1]][0]
        s0 = cols[u] - CHUNKS[c][0]
        if out and out[-1][2] == c and out[-1][3] + out[-1][1] == s0:
            out[-1] = (out[-1][0], out[-1][1] + 128, c, out[-1][3])
        else:
            out.append((128 * u, 128, c, s0))
    return out


def cut_pieces(i, g, on_vector):
    lo, hi = SHARE[2 * i + g]
    out = []
    for r0, r1 in ([(0, lo), (hi, 512)] if on_vector else [(lo, hi)]):
        for d0, wd, a, s0 in pieces(i):
            x0 = max(d0, r0)
            x1 = min(d0 + wd, r1)
            if x1 > x0:
                out.append((x0, x1 - x0, a, s0 + x0 - d0))
    return out


def producers(op):
    k = op[0]
    if k == "ex":
        return [("tx",) + op[1:]]
    if k == "qx":
        return [("ex",) + op[1:]]
    if k == "tx":
        return [("LX", op[1], op[2] // 2), ("gp",)]
    if k == "tab1":
        return [("gp",)]
    if k == "warm":
        return [("gp",)]
    if k == "sin":
        return [("tab1",), ("warm",)]
    if k == "tab2":
        return [("sin",)]
    if k in ("iv", "is"):
        return [("lw", a, op[2]) for d0, wd, a, s0 in cut_pieces(op[1], op[2], k == "iv")]
    if k == "qw":
        return [(e,) + op[1:] for e in ("iv", "is") if cut_pieces(op[1], op[2], e == "iv")]
    if k == "mm":
        return [("qx", op[2], op[3]), ("qw", op[1], 0), ("qw", op[1], 1)]
    if k == "rm":
        return [("mm",) + op[1:], ("tab2",)]
    if k == "cp":
        return [("mm",) + op[1:4]] + ([("rm",) + op[1:4]] if rotated(op[1]) else [])
    if k == "ra":
        return [("rm", op[1], op[2], m) for m in range(4)]
    if k in ("st", "sa", "sb"):
        return [("CP", op[1], op[2], m) for m in range(4)] + ([("ra", op[1], op[2])] if rotated(op[1]) else [])
    return []


def merge(lists):
    extra = {}
    pe = lists[0]
    for n in range(8, len(pe)):
        o = pe[n - 8]
        if o[0] == "tx":
            extra[pe[n]] = [("ex",) + o[1:]]
        else:
            extra[pe[n]] = [("CP",) + o[1:]] + ([("rm",) + o[1:]] if rotated(o[1]) else [])
    exs = [o for o in lists[2] if o[0] == "ex"]
    for n in range(4, len(exs)):
        extra[exs[n]] = [("qx",) + exs[n - 4][1:]]
    for i in range(len(TILES)):
        for g in range(G):
            n = 2 * i + g
            if n >= NWG:
                for k in ("iv", "is"):
                    extra[(k, i, g)] = [("qw", (n - NWG) // 2, (n - NWG) % 2)]
    idx = [0 for q in lists]
    done = set()
    out = []
    total = sum([len(q) for q in lists])
    while len(out) < total:
        progress = False
        for e in range(len(lists)):
            while idx[e] < len(lists[e]):
                op = lists[e][idx[e]]
                if not all([p in done for p in producers(op) + extra.get(op, [])]):
                    break
                out.append(op)
                done.add(op)
                if op[0] == "cp":
                    done.add(("CP",) + op[1:4])
                if op[0] == "lx":
                    for h in ([0, 1] if op[2] == 2 else [op[2]]):
                        done.add(("LX", op[1], h))
                idx[e] += 1
                progress = True
        if not progress:
            raise ValueError("the queues' orders cannot be merged: " + str([lists[e][idx[e]] for e in range(len(lists)) if idx[e] < len(lists[e])]))
    return out


def tile_gptneoxjapaneseattention_pa_kernel(tc, hidden_states, w_qkv, out_0, out_1, out_2):
    nc = tc.nc
    with ExitStack() as ctx:
        keep = ctx.enter_context(tc.tile_pool(name="keep", bufs=1))
        xg_pool = ctx.enter_context(tc.tile_pool(name="xg", bufs=4))
        wg_pool = ctx.enter_context(tc.tile_pool(name="wg", bufs=1))
        o_pool = ctx.enter_context(tc.tile_pool(name="o", bufs=9))
        bt_pool = ctx.enter_context(tc.tile_pool(name="bt", bufs=3))
        psum = ctx.enter_context(tc.psum_pool(name="psum", bufs=8))
        ctx.enter_context(tc.manual_schedule())

        zero = keep.tile([P, 1], F32, name="zero")
        warm = keep.tile([P, 1], F32, name="warm")
        ident = keep.tile([P, P], F32, name="ident")
        xraw = [keep.tile([P, MT, D], BF16, name="xraw%d" % b) for b in range(B)]
        wraw = [[keep.tile([P, 4, CHUNKS[a][1]], BF16, name="wraw%d_%d" % (a, g)) for g in range(G)] for a in range(len(CHUNKS))]
        W = MT * ROT
        pos = keep.tile([P, W], F32, name="pos")
        turns = keep.tile([P, W], F32, name="turns")
        whole_i = keep.tile([P, W], I32, name="whole_i")
        whole_f = keep.tile([P, W], F32, name="whole_f")
        frac = keep.tile([P, W], F32, name="frac")
        s_half = keep.tile([P, W], F32, name="s_half")
        s_quar = keep.tile([P, W], F32, name="s_quar")
        sq = keep.tile([P, W], F32, name="sq")
        sq2 = keep.tile([P, W], F32, name="sq2")
        c_half = keep.tile([P, W], F32, name="c_half")
        cos_t = keep.tile([P, MT, ROT], F32, name="cos_t")
        sin_t = keep.tile([P, MT, ROT], F32, name="sin_t")
        xcodes = [keep.tile([P, MT, G, P], U32, name="xcodes%d" % b, align_bytes=64) for b in range(B)]
        xscales = [keep.tile([P, MT, G, P], U8, name="xscales%d" % b, align_bytes=64) for b in range(B)]
        wcodes = [keep.tile([P, G, 512], U32, name="wcodes%d" % i, align_bytes=64) for i in range(6)]
        wscales = [keep.tile([P, G, 512], U8, name="wscales%d" % i, align_bytes=64) for i in range(6)]
        xt = {}
        xgs = {}
        wgs = {}
        pss = {}
        osbs = {}
        bts = {}

        def gp():
            nc.gpsimd.memset(zero[:], 0.0)
            nc.gpsimd.iota(pos[:], pattern=[[1, MT], [0, ROT]], base=0, channel_multiplier=MT,
                           allow_small_or_imprecise_dtypes=True)
            make_identity(nc, ident[:])

        def tab1():
            pos_v = pos[:].rearrange("p (a j) -> p a j", j=HALF)
            turns_v = turns[:].rearrange("p (a j) -> p a j", j=HALF)
            for j in range(HALF):
                c_j = 1.0 / (BASE ** (2.0 * j / ROT)) / (2.0 * math.pi)
                nc.vector.tensor_scalar(out=turns_v[:, :, j : j + 1], in0=pos_v[:, :, j : j + 1],
                                        scalar1=c_j, scalar2=None, op0=ALU.mult)
            nc.vector.tensor_copy(out=whole_i[:], in_=turns[:])
            nc.vector.tensor_copy(out=whole_f[:], in_=whole_i[:])
            nc.vector.tensor_tensor(out=frac[:], in0=turns[:], in1=whole_f[:], op=ALU.subtract)

        def sins():
            nc.scalar.activation(out=s_half[:], in_=frac[:], func=ACT.Sin, scale=math.pi)
            nc.scalar.activation(out=s_quar[:], in_=frac[:], func=ACT.Sin, scale=math.pi / 2.0)

        def tab2():
            nc.vector.tensor_tensor(out=sq[:], in0=s_half[:], in1=s_half[:], op=ALU.mult)
            nc.vector.tensor_tensor(out=sq2[:], in0=s_quar[:], in1=s_quar[:], op=ALU.mult)
            nc.vector.tensor_scalar(out=cos_t[:].rearrange("p m r -> p (m r)"), in0=sq[:],
                                    scalar1=-2.0, scalar2=1.0, op0=ALU.mult, op1=ALU.add)
            nc.vector.tensor_scalar(out=c_half[:], in0=sq2[:], scalar1=-2.0, scalar2=1.0, op0=ALU.mult, op1=ALU.add)
            sh_v = s_half[:].rearrange("p (m h j) -> p m h j", m=MT, h=2)
            ch_v = c_half[:].rearrange("p (m h j) -> p m h j", m=MT, h=2)
            st_v = sin_t[:].rearrange("p m (h j) -> p m h j", h=2)
            for h, sign in ((0, 2.0), (1, -2.0)):
                nc.vector.scalar_tensor_tensor(out=st_v[:, :, h, :], in0=sh_v[:, :, h, :], scalar=sign,
                                               in1=ch_v[:, :, h, :], op0=ALU.mult, op1=ALU.mult)

        def lx(b, h):
            src = hidden_states[b].rearrange("(p m) k -> p m k", m=MT)
            if h == 2:
                nc.sync.dma_start(out=xraw[b][:], in_=src)
            else:
                nc.sync.dma_start(out=xraw[b][:, 2 * h : 2 * h + 2, :], in_=src[:, 2 * h : 2 * h + 2, :])

        def lw(a, g):
            nc.sync.dma_start(
                out=wraw[a][g][:],
                in_=w_qkv[512 * g : 512 * (g + 1), CHUNKS[a][0] : CHUNKS[a][0] + CHUNKS[a][1]].rearrange("(p j) w -> p j w", j=4),
            )

        def tx(b, m):
            words = xraw[b][:, m, :].bitcast(F32)
            t = psum.tile([P, G, 2, P], F32, tag="bank", name="xt")
            for g in range(G):
                for u in range(2):
                    nc.tensor.transpose(t[:, g, u, :], words[:, 256 * g + u : 256 * (g + 1) : 2], ident[:])
            xt[(b, m)] = t

        def ex(b, m):
            xg = xg_pool.tile([P, G, P, 4], BF16, name="xg", align_bytes=64)
            nc.scalar.copy(out=xg[:].bitcast(F32), in_=xt[(b, m)][:].rearrange("p g u r -> p g r u"))
            xgs[(b, m)] = xg

        def qx(b, m):
            nc.vector.quantize_mx(
                out=xcodes[b][:, m].rearrange("p g r -> p (g r)").bitcast(FP8X4),
                scales=xscales[b][:, m].rearrange("p g r -> p (g r)"),
                in_=xgs[(b, m)][:].rearrange("p g r t -> p (g r t)"),
            )

        def interleave(i, g, on_vector):
            if (i, g) not in wgs:
                wgs[(i, g)] = wg_pool.tile([P, 512, 4], BF16, name="wg%d" % ((2 * i + g) % NWG), align_bytes=64)
            wg = wgs[(i, g)]
            for d0, wd, a, s0 in cut_pieces(i, g, on_vector):
                dst = wg[:, d0 : d0 + wd, :].rearrange("p (c i) j -> p c j i", i=4)
                src = wraw[a][g][:, :, s0 : s0 + wd].rearrange("p j (c i) -> p c j i", i=4)
                if on_vector:
                    nc.vector.tensor_copy(out=dst, in_=src)
                else:
                    nc.scalar.copy(out=dst, in_=src)

        def qw(i, g):
            nc.vector.quantize_mx(
                out=wcodes[i][:, g, :].bitcast(FP8X4),
                scales=wscales[i][:, g, :],
                in_=wgs[(i, g)][:].rearrange("p w j -> p (w j)"),
            )

        def mm(i, b, m):
            ps = psum.tile([P, 4, HS], F32, tag="bank", name="ps")
            for g in range(G):
                nc.tensor.matmul_mx(
                    out=ps[:].rearrange("p u f -> p (u f)"),
                    lhsT=xcodes[b][:, m, g, :].bitcast(FP8X4),
                    lhsT_scale=xscales[b][:, m, g, :],
                    rhs=wcodes[i][:, g, :].bitcast(FP8X4),
                    rhs_scale=wscales[i][:, g, :],
                    start=(g == 0),
                    stop=(g == G - 1),
                )
            pss[(i, b, m)] = ps

        def osb_of(i, b):
            if (i, b) not in osbs:
                osbs[(i, b)] = o_pool.tile([P, 4, MT, HS], F32, name="osb")
            return osbs[(i, b)]

        def rm(i, b, m):
            osb = osb_of(i, b)
            if (i, b) not in bts:
                bts[(i, b)] = bt_pool.tile([P, 4, MT, ROT], F32, name="bt")
            ps = pss[(i, b, m)]
            nc.vector.tensor_tensor(out=osb[:, :, m, 0:ROT], in0=ps[:, :, 0:ROT],
                                    in1=cos_t[:, m : m + 1, :].to_broadcast([P, 4, ROT]), op=ALU.mult)
            nc.vector.tensor_tensor(out=bts[(i, b)][:, :, m, :], in0=ps[:, :, 0:ROT],
                                    in1=sin_t[:, m : m + 1, :].to_broadcast([P, 4, ROT]), op=ALU.mult)

        def cp(i, b, m, eng):
            osb = osb_of(i, b)
            ps = pss[(i, b, m)]
            lo = ROT if rotated(i) else 0
            if eng == "S":
                nc.scalar.copy(out=osb[:, :, m, lo:HS], in_=ps[:, :, lo:HS])
            else:
                nc.vector.tensor_copy(out=osb[:, :, m, lo:HS], in_=ps[:, :, lo:HS])

        def ra(i, b):
            osb = osbs[(i, b)]
            bt = bts[(i, b)]
            nc.vector.tensor_tensor(out=osb[:, :, :, 0:HALF], in0=osb[:, :, :, 0:HALF],
                                    in1=bt[:, :, :, HALF:ROT], op=ALU.add)
            nc.vector.tensor_tensor(out=osb[:, :, :, HALF:ROT], in0=osb[:, :, :, HALF:ROT],
                                    in1=bt[:, :, :, 0:HALF], op=ALU.add)

        def st(i, b, parts, queue):
            kind, a = TILES[i]
            osb = osbs[(i, b)]
            if kind == "qk":
                by_kind = osb[:].rearrange("p (hh s) m f -> p s hh (m f)", s=2)
                for s in parts:
                    queue.dma_start(out=(out_0, out_1)[s][b, 2 * a : 2 * a + 2].rearrange("h (p m) f -> p h (m f)", m=MT),
                                    in_=by_kind[:, s])
            elif len(parts) == 2:
                dst = (out_0, out_1, out_2)[KINDS[kind]]
                queue.dma_start(out=dst[b, 4 * a : 4 * a + 4].rearrange("h (p m) f -> p h (m f)", m=MT),
                                in_=osb[:].rearrange("p u m f -> p u (m f)"))
            else:
                dst = (out_0, out_1, out_2)[KINDS[kind]]
                h0 = 2 * parts[0]
                queue.dma_start(out=dst[b, 4 * a + h0 : 4 * a + h0 + 2].rearrange("h (p m) f -> p h (m f)", m=MT),
                                in_=osb[:, h0 : h0 + 2].rearrange("p u m f -> p u (m f)"))

        for op in merge([parse(Q_PE), parse(Q_V), parse(Q_S), parse(Q_SP), [("gp",)]]):
            k = op[0]
            if k == "gp":
                gp()
            elif k == "warm":
                nc.scalar.activation(out=warm[:], in_=zero[:], func=ACT.Sin)
            elif k == "tab1":
                tab1()
            elif k == "sin":
                sins()
            elif k == "tab2":
                tab2()
            elif k == "lx":
                lx(op[1], op[2])
            elif k == "lw":
                lw(op[1], op[2])
            elif k == "tx":
                tx(op[1], op[2])
            elif k == "ex":
                ex(op[1], op[2])
            elif k == "qx":
                qx(op[1], op[2])
            elif k == "iv":
                interleave(op[1], op[2], True)
            elif k == "is":
                interleave(op[1], op[2], False)
            elif k == "qw":
                qw(op[1], op[2])
            elif k == "mm":
                mm(op[1], op[2], op[3])
            elif k == "rm":
                rm(op[1], op[2], op[3])
            elif k == "cp":
                cp(op[1], op[2], op[3], op[4])
            elif k == "ra":
                ra(op[1], op[2])
            elif k == "st":
                st(op[1], op[2], (0, 1), nc.sync)
            elif k == "sa":
                st(op[1], op[2], (0,), nc.sync)
            elif k == "sb":
                st(op[1], op[2], (1,), nc.scalar)
            else:
                raise ValueError(k)
